import numpy as np
import ml_dtypes


def mxq(x, axis, fmt="e4m3"):
    dtype, down = {"e4m3": (ml_dtypes.float8_e4m3fn, 7), "e5m2": (ml_dtypes.float8_e5m2, 14)}[fmt]
    v = np.moveaxis(np.asarray(x, np.float32).astype(ml_dtypes.bfloat16).astype(np.float64), axis, -1)
    blocks = v.reshape(v.shape[:-1] + (-1, 32))
    amax = np.abs(blocks).max(-1, keepdims=True)
    byte = np.maximum(np.where(amax > 0, np.frexp(amax)[1] - 1 + 127, 0) - down, 1)
    scale = np.exp2(byte - 127.0)
    codes = (blocks / scale).astype(np.float32).astype(dtype).astype(np.float64)
    return np.moveaxis((codes * scale).reshape(v.shape), -1, axis)


WIDE = False


def mx_kscale(k):
    if not WIDE:
        return np.ones(k)
    levels = np.array([30, -30])
    if k % 512:
        return np.exp2(np.random.permutation(np.resize(levels, k // 32))).repeat(32)
    a = np.empty((k // 512, 16))
    for p in range(k // 512):
        a[p, :8] = np.random.permutation(np.resize(levels, 8))
        for g in range(8):
            far = levels[np.abs(levels - a[p, g]) >= 10]
            a[p, g + 8] = far[np.random.randint(len(far))]
    return np.exp2(a.ravel()).repeat(32)


BF16 = ml_dtypes.bfloat16


def bf(x):
    return np.asarray(x, np.float32).astype(BF16)


def f64(x):
    return np.asarray(x).astype(np.float64)


E2M1 = np.array([0.0, 0.5, 1.0, 1.5, 2.0, 3.0, 4.0, 6.0, -0.0, -0.5, -1.0, -1.5, -2.0, -3.0, -4.0, -6.0])


def pack_weight(w, fmt):
    k, n = w.shape
    w = f64(bf(w)).reshape(k // 32, 32, n)
    amax = np.abs(w).max(1)
    if fmt == "e4m3":
        byte = np.frexp(amax)[1] - 1 + 127 - 7
    else:
        mant, ex = np.frexp(amax / 6.0)
        byte = np.where(mant > 0.5, ex, ex - 1) + 127
    byte = np.clip(np.where(amax > 0, byte, 1), 1, 254)
    scaled = (w * np.exp2(127.0 - byte)[:, None, :]).reshape(k, n).astype(np.float32)
    by_word = np.ascontiguousarray(scaled.reshape(k // 512, 128, 4, n).transpose(0, 1, 3, 2))
    if fmt == "e4m3":
        words = by_word.astype(ml_dtypes.float8_e4m3fn).view(np.uint8)
    else:
        c = by_word.astype(ml_dtypes.float4_e2m1fn).view(np.uint8) & 0xF
        words = c[..., 0::2] | (c[..., 1::2] << 4)
    return np.ascontiguousarray(words), np.ascontiguousarray(byte.astype(np.uint8).reshape(k // 512, 16, n))


def unpack_weight(words, scales, fmt):
    g, p, n, _ = words.shape
    if fmt == "e4m3":
        vals = np.ascontiguousarray(words).view(ml_dtypes.float8_e4m3fn).astype(np.float64)
    else:
        nib = np.empty((g, p, n, 4), np.uint8)
        nib[..., 0::2] = words & 0xF
        nib[..., 1::2] = words >> 4
        vals = E2M1[nib]
    vals = vals * np.repeat(np.exp2(scales.astype(np.float64) - 127.0), 8, axis=1)[..., None]
    return vals.transpose(0, 1, 3, 2).reshape(g * 512, n)

def pack4(w):
    words, scales = pack_weight(w, "e2m1")
    return words.reshape(words.shape[0], 128, -1), scales


def unpack4(words, scales):
    return unpack_weight(words.reshape(words.shape[0], 128, -1, 2), scales, "e2m1")


B, T, C, NH, G, HS, K, WIN = 1, 1024, 1024, 16, 4, 128, 4, 512
QPK = NH // G


def silu(v):
    return v / (1.0 + np.exp(-v))


def causal_conv1d_silu(u, w):
    up = np.pad(u, ((0, 0), (K - 1, 0), (0, 0)))
    out = sum(w[None, None, :, j] * up[:, j:j + T, :] for j in range(K))
    return silu(out)


def apply_rope(u, cos, sin):
    d = cos.shape[-1]
    u1, u2 = u[..., :d], u[..., d:]
    c = cos[None, :, None, :]
    s = sin[None, :, None, :]
    return np.concatenate([u1 * c - u2 * s, u1 * s + u2 * c], axis=-1)


def setup_inputs():
    s = mx_kscale(C)
    theta = 1.0 / (10000.0 ** (np.arange(0, HS, 2) / HS))
    idx = np.outer(np.arange(T), theta)
    x = bf(np.random.standard_normal((B, T, C)) * s)
    words, scales = pack4(np.random.standard_normal((C, (NH + 2 * G) * HS)) * 2.0 / np.sqrt(C) / s[:, None])
    return {"x": x,
            "Wqkv_words": words, "Wqkv_scales": scales,
            "q_conv_w": bf(np.random.standard_normal((NH * HS, K)) * 0.5),
            "k_conv_w": bf(np.random.standard_normal((G * HS, K)) * 0.5),
            "v_conv_w": bf(np.random.standard_normal((G * HS, K)) * 0.5),
            "cos": bf(np.cos(idx)), "sin": bf(np.sin(idx))}


def reference(x, Wqkv_words, Wqkv_scales, q_conv_w, k_conv_w, v_conv_w, cos, sin):
    qkv = (mxq(f64(x).reshape(B * T, C), 1, "e5m2") @ unpack4(Wqkv_words, Wqkv_scales)).reshape(B, T, G, QPK + 2, HS)
    q = qkv[..., :QPK, :].reshape(B, T, NH * HS)
    k = qkv[..., QPK:QPK + 1, :].reshape(B, T, G * HS)
    v = qkv[..., QPK + 1:, :].reshape(B, T, G * HS)
    q = causal_conv1d_silu(q, f64(q_conv_w)).reshape(B, T, NH, HS)
    k = causal_conv1d_silu(k, f64(k_conv_w)).reshape(B, T, G, HS)
    v = causal_conv1d_silu(v, f64(v_conv_w)).reshape(B, T, G, HS)
    q = apply_rope(q, f64(cos), f64(sin))
    k = apply_rope(k, f64(cos), f64(sin))
    return q, k, v

@@ -1,0 +1,308 @@
+from contextlib import ExitStack
+
+import concourse.mybir as mybir
+from concourse.masks import make_identity
+
+T, C = 1024, 1024
+GROUPS, HEADS_PER_GROUP, HS = 4, 6, 128
+HEADS = GROUPS * HEADS_PER_GROUP
+FLOPS = 2 * T * C * HEADS * HS
+
+F32 = mybir.dt.float32
+BF16 = mybir.dt.bfloat16
+I32 = mybir.dt.int32
+U32 = mybir.dt.uint32
+U8 = mybir.dt.uint8
+E5M2X4 = mybir.dt.float8_e5m2_x4
+E2M1X4 = mybir.dt.float4_e2m1fn_x4
+ALU = mybir.AluOpType
+ACT = mybir.ActivationFunctionType
+
+P = 128
+PASSES = C // 512
+HALF = 512
+TILES = T // P
+TILES_PER_HALF = HALF // P
+ROT = HS // 2
+
+EARLY_HEADS = 4
+CONV_BUFS = 4
+Y_BUFS = 6
+ROPE_BUFS = 4
+MX_BANKS = 3
+TR_BANKS = 4
+COS_EVERY = 5
+COS_PHASE = 3
+TAIL_COS = 1
+TAIL_ADD = 1
+THIRD_LAST = 0
+THIRD_SKIP = 0
+SPLIT_LAST = 0
+LAST_VALUES = 1
+LATE_ON_SCALAR = 2
+
+
+def tile_gpt_pa_kernel(tc, x, w_words, w_scales, q_conv_w, k_conv_w, v_conv_w, cos, sin, out_q, out_k, out_v):
+    nc = tc.nc
+    with ExitStack() as ctx:
+        sb = ctx.enter_context(tc.tile_pool(name="sb", bufs=1))
+        ps = ctx.enter_context(tc.psum_pool(name="ps", bufs=1))
+        ctx.enter_context(tc.manual_schedule())
+
+        def tiles(pool, name, count, shape, dtype):
+            return [pool.tile(shape, dtype, name="%s%d" % (name, i), align_bytes=64) for i in range(count)]
+
+        x_rows = tiles(sb, "x_rows", TILES, [P, C], BF16)
+        x_t = tiles(sb, "x_t", 2, [P, PASSES, 4 * HALF], BF16)
+        x_codes = tiles(sb, "x_codes", 2, [P, PASSES, HALF], U32)
+        x_scales = tiles(sb, "x_scales", 2, [P, PASSES, HALF], U8)
+        group_cols = HEADS_PER_GROUP * HS
+        w_codes = tiles(sb, "w_codes", GROUPS, [P, PASSES, 2 * group_cols], U8)
+        plane_first = sb.tile([P, PASSES, group_cols], U8, align_bytes=64)
+        plane_rest = sb.tile([P, PASSES, (GROUPS - 1) * group_cols], U8, align_bytes=64)
+        tap_rows = sb.tile([P, 4 * HS], BF16, align_bytes=64)
+        taps = sb.tile([P, 4, HEADS], F32, align_bytes=64)
+        cos_sb = sb.tile([P, TILES, ROT], BF16, align_bytes=64)
+        sin_sb = sb.tile([P, TILES, ROT], BF16, align_bytes=64)
+        ident_f32 = sb.tile([P, P], F32, align_bytes=64)
+        ident_bf = sb.tile([P, P], BF16, align_bytes=64)
+        prod0 = tiles(sb, "prod0", CONV_BUFS, [P, T], F32)
+        prod2 = tiles(sb, "prod2", CONV_BUFS, [P, T], F32)
+        pair01 = tiles(sb, "pair01", CONV_BUFS, [P, T], F32)
+        pair23 = tiles(sb, "pair23", CONV_BUFS, [P, T], F32)
+        y_bufs = tiles(sb, "y", Y_BUFS, [P, TILES, HS], F32)
+        y_cos = tiles(sb, "y_cos", ROPE_BUFS, [P, TILES, HS], F32)
+        y_sin = tiles(sb, "y_sin", ROPE_BUFS, [P, TILES, HS], F32)
+        rotated = tiles(sb, "rotated", ROPE_BUFS, [P, TILES, HS], F32)
+
+        mx_banks = [ps.tile([P, HALF], F32, name="mx%d" % i) for i in range(MX_BANKS)]
+        tr_banks = [ps.tile([P, HALF], F32, name="tr%d" % i) for i in range(TR_BANKS)]
+        tables = ps.tile([P, 2, TILES, ROT], BF16)
+
+        nc.vector.memset(plane_first[:].bitcast(I32), 0)
+        nc.vector.memset(tap_rows[:].bitcast(I32), 0)
+        make_identity(nc, ident_f32[:])
+        nc.vector.memset(plane_rest[:].bitcast(I32), 0)
+        for i in range(CONV_BUFS):
+            nc.vector.memset(prod0[i][:, 0:1], 0.0)
+            nc.vector.memset(prod2[i][:, 0:1], 0.0)
+            nc.vector.memset(pair01[i][:, 0:2], 0.0)
+
+        def load_x(i):
+            nc.sync.dma_start(out=x_rows[i][:], in_=x[0, P * i : P * (i + 1), :])
+
+        def load_w(g):
+            src = w_words.rearrange("g p n -> p g n")[:, :, 2 * group_cols * g : 2 * group_cols * (g + 1)]
+            nc.sync.dma_start(out=w_codes[g][:].bitcast(I32), in_=src.bitcast(I32))
+
+        def load_plane(queue, plane, lo, hi):
+            for q in range(4):
+                queue.dma_start(
+                    out=plane[32 * q : 32 * q + 4, :, :].bitcast(I32),
+                    in_=w_scales[:, 4 * q : 4 * q + 4, lo:hi].rearrange("g r n -> r g n").bitcast(I32),
+                )
+
+        for i in range(TILES_PER_HALF):
+            load_x(i)
+        load_plane(nc.sync, plane_first, 0, group_cols)
+        load_w(0)
+        first = 0
+        for conv_w in (q_conv_w, k_conv_w, v_conv_w):
+            n = conv_w.shape[0] // HS
+            nc.gpsimd.dma_start(out=tap_rows[first : first + n, :], in_=conv_w.rearrange("(h c) j -> h (c j)", c=HS))
+            first += n
+        make_identity(nc, ident_bf[:])
+        for i in range(TILES_PER_HALF, TILES):
+            load_x(i)
+        nc.sync.dma_start(out=cos_sb[:], in_=cos.rearrange("(i p) d -> p i d", p=P))
+        nc.sync.dma_start(out=sin_sb[:], in_=sin.rearrange("(i p) d -> p i d", p=P))
+        load_plane(nc.sync, plane_rest, group_cols, GROUPS * group_cols)
+        for g in range(1, GROUPS):
+            load_w(g)
+
+        counters = {"mx": 0, "tr": 0, "rope": 0}
+
+        def take(kind, bufs):
+            buf = bufs[counters[kind] % len(bufs)]
+            counters[kind] += 1
+            return buf
+
+        def transpose_x(i):
+            bank = take("tr", tr_banks)
+            words = x_rows[i][:].bitcast(F32)
+            for g in range(PASSES):
+                for u in range(2):
+                    col = P * (2 * g + u)
+                    nc.tensor.transpose(bank[:, col : col + P], words[:, 256 * g + u : 256 * (g + 1) : 2], ident_f32[:])
+            return bank
+
+        def copy_x(i, bank, on_scalar):
+            half, j = divmod(i, TILES_PER_HALF)
+            dst = x_t[half][:].bitcast(F32).rearrange("p g (t u) -> p g t u", u=2)[:, :, P * j : P * (j + 1), :]
+            src = bank[:].rearrange("p (g u t) -> p g t u", g=PASSES, u=2)
+            if on_scalar:
+                nc.scalar.copy(out=dst, in_=src)
+            else:
+                nc.vector.tensor_copy(out=dst, in_=src)
+
+        def quantize_x(half, g):
+            nc.vector.quantize_mx(out=x_codes[half][:, g, :].bitcast(E5M2X4), scales=x_scales[half][:, g, :], in_=x_t[half][:, g, :])
+
+        def kind_of(h):
+            g, j = divmod(h, HEADS_PER_GROUP)
+            if j < 4:
+                return out_q, 4 * g + j, 4 * g + j
+            if j == 4:
+                return out_k, g, 16 + g
+            return out_v, g, 20 + g
+
+        def project(h, half):
+            g, j = divmod(h, HEADS_PER_GROUP)
+            bank = take("mx", mx_banks)
+            for c in range(PASSES):
+                nc.tensor.matmul_mx(
+                    out=bank[:],
+                    lhsT=w_codes[g][:, c, 2 * HS * j : 2 * HS * (j + 1)].bitcast(E2M1X4),
+                    lhsT_scale=plane_first[:, c, HS * h : HS * (h + 1)] if g == 0 else plane_rest[:, c, HS * h - group_cols : HS * (h + 1) - group_cols],
+                    rhs=x_codes[half][:, c, :].bitcast(E5M2X4),
+                    rhs_scale=x_scales[half][:, c, :],
+                    start=(c == 0),
+                    stop=(c == PASSES - 1),
+                )
+            return bank
+
+        def tap(h, j):
+            row = kind_of(h)[2]
+            return taps[:, j, row : row + 1]
+
+        def three_terms(h, half):
+            return len(units) - THIRD_SKIP > units.index((h, half)) >= len(units) - THIRD_LAST - THIRD_SKIP
+
+        def conv_products(h, half, u):
+            t0 = HALF * half
+            n = min(HALF, T - t0 - 1)
+            for buf, j in ((prod0, 0), (prod2, 2)):
+                nc.scalar.activation(out=buf[slot[h] % CONV_BUFS][:, t0 + 1 : t0 + 1 + n], in_=u[:, 0:n], func=ACT.Copy, scale=tap(h, j))
+            if three_terms(h, half):
+                nc.scalar.activation(out=pair23[slot[h] % CONV_BUFS][:, t0 : t0 + HALF], in_=u[:], func=ACT.Copy, scale=tap(h, 3))
+
+        def conv_pairs(h, half, u):
+            t0 = HALF * half
+            b = slot[h] % CONV_BUFS
+            n = min(HALF, T - t0 - 2)
+            nc.vector.scalar_tensor_tensor(
+                out=pair01[b][:, t0 + 2 : t0 + 2 + n], in0=u[:, 0:n], scalar=tap(h, 1), in1=prod0[b][:, t0 : t0 + n], op0=ALU.mult, op1=ALU.add
+            )
+            if not three_terms(h, half):
+                nc.vector.scalar_tensor_tensor(
+                    out=pair23[b][:, t0 : t0 + HALF], in0=u[:], scalar=tap(h, 3), in1=prod2[b][:, t0 : t0 + HALF], op0=ALU.mult, op1=ALU.add
+                )
+
+        def transpose_sum(h, half):
+            bank = take("tr", tr_banks)
+            b = slot[h] % CONV_BUFS
+            terms = [pair01, pair23] + ([prod2] if three_terms(h, half) else [])
+            for j in range(TILES_PER_HALF):
+                t0 = HALF * half + P * j
+                for n, term in enumerate(terms):
+                    nc.tensor.matmul(
+                        bank[:, P * j : P * (j + 1)], lhsT=term[b][:, t0 : t0 + P], rhs=ident_f32[:], start=(n == 0), stop=(n == len(terms) - 1), is_transpose=True
+                    )
+            return bank
+
+        def silu(h, half, bank):
+            lo = TILES_PER_HALF * half
+            nc.scalar.activation(
+                out=y_bufs[slot[h] % Y_BUFS][:, lo : lo + TILES_PER_HALF, :], in_=bank[:].rearrange("p (i d) -> p i d", d=HS), func=ACT.Silu
+            )
+
+        def store(h, lo, hi, src):
+            out, head, unused = kind_of(h)
+            queue = nc.scalar if slot[h] == HEADS - 1 else nc.sync
+            queue.dma_start(out=out[0].rearrange("(i p) h d -> p i h d", p=P)[:, lo:hi, head, :], in_=src[:, lo:hi, :])
+
+        def both_halves(table):
+            return table.rearrange("p i (o d) -> p i o d", o=1).to_broadcast([P, table.shape[1], 2, ROT])
+
+        def cos_product(engine, table, h, lo, hi, b):
+            engine.tensor_tensor(
+                out=y_cos[b][:, lo:hi, :].rearrange("p i (o d) -> p i o d", o=2),
+                in0=y_bufs[slot[h] % Y_BUFS][:, lo:hi, :].rearrange("p i (o d) -> p i o d", o=2),
+                in1=both_halves(table[:, lo:hi, :]),
+                op=ALU.mult,
+            )
+
+        def sin_product(h, lo, hi, b):
+            y = y_bufs[slot[h] % Y_BUFS]
+            s = tables[:, 1, lo:hi, :]
+            nc.vector.scalar_tensor_tensor(out=y_sin[b][:, lo:hi, 0:ROT], in0=y[:, lo:hi, ROT:HS], scalar=-1.0, in1=s, op0=ALU.mult, op1=ALU.mult)
+            nc.vector.tensor_tensor(out=y_sin[b][:, lo:hi, ROT:HS], in0=y[:, lo:hi, 0:ROT], in1=s, op=ALU.mult)
+
+        def rope_add(engine, h, lo, hi, b):
+            engine.tensor_tensor(out=rotated[b][:, lo:hi, :], in0=y_cos[b][:, lo:hi, :], in1=y_sin[b][:, lo:hi, :], op=ALU.add)
+            store(h, lo, hi, rotated[b])
+
+        def jobs(pair):
+            (h0, a), (h1, b) = pair
+            if h0 == h1 and slot[h0] < HEADS - SPLIT_LAST:
+                return [(h0, 0, TILES)]
+            return [(h, TILES_PER_HALF * half, TILES_PER_HALF * (half + 1)) for h, half in pair]
+
+        values = [h for h in range(HEADS) if h % HEADS_PER_GROUP == 5]
+        order = [h for h in range(HEADS) if h not in values[GROUPS - LAST_VALUES :]] + values[GROUPS - LAST_VALUES :]
+        roped = [h for h in order if h not in values]
+        slot = {h: i for i, h in enumerate(order)}
+        units = [(h, half) for half in range(2) for h in order[:EARLY_HEADS]]
+        units += [(h, half) for h in order[EARLY_HEADS:] for half in range(2)]
+        pairs = [units[i : i + 2] for i in range(0, len(units), 2)]
+
+        for i in range(TILES_PER_HALF):
+            copy_x(i, transpose_x(i), on_scalar=(i % 2 == 0))
+        flat_tables = tables[:].rearrange("p s i d -> p (s i d)")
+        for j in range(4):
+            nc.tensor.transpose(flat_tables[:, P * j : P * (j + 1)], tap_rows[:, j : 4 * HS : 4], ident_bf[:])
+        nc.scalar.activation(out=taps[:], in_=flat_tables[:, 0 : 4 * P].rearrange("p (j h) -> p j h", j=4)[:, :, 0:HEADS], func=ACT.Copy)
+        for g in range(PASSES):
+            quantize_x(0, g)
+        for i in range(TILES_PER_HALF, TILES_PER_HALF + LATE_ON_SCALAR):
+            copy_x(i, transpose_x(i), on_scalar=True)
+
+        for k in range(len(pairs) + 2):
+            current = pairs[k] if k < len(pairs) else []
+            before = pairs[k - 1] if 1 <= k <= len(pairs) else []
+            sums = [project(h, half) for h, half in current]
+            late_x = [(i, transpose_x(i)) for i in range(TILES_PER_HALF + LATE_ON_SCALAR, TILES)] if k == 0 else []
+            if k == 1:
+                for i, table in enumerate((cos_sb, sin_sb)):
+                    nc.tensor.matmul(
+                        tables[:, i].rearrange("p i d -> p (i d)"), lhsT=ident_bf[:], rhs=table[:].rearrange("p i d -> p (i d)"), start=True, stop=True
+                    )
+            turned = [transpose_sum(h, half) for h, half in before]
+            todo = jobs(pairs[k - 2]) if k >= 2 else []
+            after = []
+            for h, lo, hi in todo:
+                if h in values:
+                    continue
+                job = (h, lo, hi, counters["rope"] % ROPE_BUFS)
+                counters["rope"] += 1
+                sin_product(*job)
+                r = roped.index(h)
+                if r >= len(roped) - TAIL_COS or r % COS_EVERY == COS_PHASE:
+                    cos_product(nc.vector, tables[:, 0], *job)
+                else:
+                    cos_product(nc.gpsimd, cos_sb, *job)
+                after.append(job)
+            for i, bank in late_x:
+                copy_x(i, bank, on_scalar=False)
+            for n, (h, half) in enumerate(current):
+                conv_products(h, half, sums[n])
+                conv_pairs(h, half, sums[n])
+                if k == 0 and n == 0:
+                    for g in range(PASSES):
+                        quantize_x(1, g)
+            for job in after:
+                rope_add(nc.vector if roped.index(job[0]) >= len(roped) - TAIL_ADD else nc.gpsimd, *job)
+            for (h, half), bank in zip(before, turned):
+                silu(h, half, bank)
+                if h % HEADS_PER_GROUP == 5:
+                    store(h, TILES_PER_HALF * half, TILES_PER_HALF * (half + 1), y_bufs[slot[h] % Y_BUFS])

@@ -29,16 +29,18 @@ EARLY_HEADS = 4
 CONV_BUFS = 4
 Y_BUFS = 6
 ROPE_BUFS = 4
-MX_BANKS = 3
-TR_BANKS = 4
+MX_BANKS = 4
+TR_BANKS = 3
 COS_EVERY = 5
 COS_PHASE = 3
-TAIL_COS = 1
-TAIL_ADD = 1
-THIRD_LAST = 0
-THIRD_SKIP = 0
+TAIL_COS = 0
+TAIL_ADD = 0
+THIRD_J = 3
+COS_J = (1, 3)
+HEAD_COS = 0
+ROPE_LAST = 0
 SPLIT_LAST = 0
-LAST_VALUES = 1
+LAST_VALUES = 3
 LATE_ON_SCALAR = 2
 
 
@@ -64,6 +66,7 @@ def tile_gpt_pa_kernel(tc, x, w_words, w_scales, q_conv_w, k_conv_w, v_conv_w, c
         taps = sb.tile([P, 4, HEADS], F32, align_bytes=64)
         cos_sb = sb.tile([P, TILES, ROT], BF16, align_bytes=64)
         sin_sb = sb.tile([P, TILES, ROT], BF16, align_bytes=64)
+        cos_wide = sb.tile([P, TILES, HS], F32, align_bytes=64)
         ident_f32 = sb.tile([P, P], F32, align_bytes=64)
         ident_bf = sb.tile([P, P], BF16, align_bytes=64)
         prod0 = tiles(sb, "prod0", CONV_BUFS, [P, T], F32)
@@ -111,7 +114,7 @@ def tile_gpt_pa_kernel(tc, x, w_words, w_scales, q_conv_w, k_conv_w, v_conv_w, c
             n = conv_w.shape[0] // HS
             nc.gpsimd.dma_start(out=tap_rows[first : first + n, :], in_=conv_w.rearrange("(h c) j -> h (c j)", c=HS))
             first += n
-        make_identity(nc, ident_bf[:])
+        nc.scalar.activation(out=ident_bf[:], in_=ident_f32[:], func=ACT.Copy)
         for i in range(TILES_PER_HALF, TILES):
             load_x(i)
         nc.sync.dma_start(out=cos_sb[:], in_=cos.rearrange("(i p) d -> p i d", p=P))
@@ -176,7 +179,7 @@ def tile_gpt_pa_kernel(tc, x, w_words, w_scales, q_conv_w, k_conv_w, v_conv_w, c
             return taps[:, j, row : row + 1]
 
         def three_terms(h, half):
-            return len(units) - THIRD_SKIP > units.index((h, half)) >= len(units) - THIRD_LAST - THIRD_SKIP
+            return (h % HEADS_PER_GROUP, half) == (THIRD_J, 1)
 
         def conv_products(h, half, u):
             t0 = HALF * half
@@ -218,19 +221,23 @@ def tile_gpt_pa_kernel(tc, x, w_words, w_scales, q_conv_w, k_conv_w, v_conv_w, c
 
         def store(h, lo, hi, src):
             out, head, unused = kind_of(h)
-            queue = nc.scalar if slot[h] == HEADS - 1 else nc.sync
+            queue = nc.scalar if slot[h] >= HEADS - LAST_VALUES else nc.sync
             queue.dma_start(out=out[0].rearrange("(i p) h d -> p i h d", p=P)[:, lo:hi, head, :], in_=src[:, lo:hi, :])
 
         def both_halves(table):
             return table.rearrange("p i (o d) -> p i o d", o=1).to_broadcast([P, table.shape[1], 2, ROT])
 
-        def cos_product(engine, table, h, lo, hi, b):
-            engine.tensor_tensor(
-                out=y_cos[b][:, lo:hi, :].rearrange("p i (o d) -> p i o d", o=2),
-                in0=y_bufs[slot[h] % Y_BUFS][:, lo:hi, :].rearrange("p i (o d) -> p i o d", o=2),
-                in1=both_halves(table[:, lo:hi, :]),
-                op=ALU.mult,
-            )
+        def cos_product(on_vector, h, lo, hi, b):
+            y = y_bufs[slot[h] % Y_BUFS][:, lo:hi, :]
+            if on_vector:
+                nc.vector.tensor_tensor(
+                    out=y_cos[b][:, lo:hi, :].rearrange("p i (o d) -> p i o d", o=2),
+                    in0=y.rearrange("p i (o d) -> p i o d", o=2),
+                    in1=both_halves(tables[:, 0, lo:hi, :]),
+                    op=ALU.mult,
+                )
+            else:
+                nc.gpsimd.tensor_tensor(out=y_cos[b][:, lo:hi, :], in0=y, in1=cos_wide[:, lo:hi, :], op=ALU.mult)
 
         def sin_product(h, lo, hi, b):
             y = y_bufs[slot[h] % Y_BUFS]
@@ -267,6 +274,9 @@ def tile_gpt_pa_kernel(tc, x, w_words, w_scales, q_conv_w, k_conv_w, v_conv_w, c
         for i in range(TILES_PER_HALF, TILES_PER_HALF + LATE_ON_SCALAR):
             copy_x(i, transpose_x(i), on_scalar=True)
 
+        nc.gpsimd.tensor_scalar(
+            out=cos_wide[:].rearrange("p i (o d) -> p i o d", o=2), in0=both_halves(cos_sb[:]), scalar1=1.0, scalar2=0.0, op0=ALU.mult, op1=ALU.add
+        )
         for k in range(len(pairs) + 2):
             current = pairs[k] if k < len(pairs) else []
             before = pairs[k - 1] if 1 <= k <= len(pairs) else []
@@ -280,6 +290,12 @@ def tile_gpt_pa_kernel(tc, x, w_words, w_scales, q_conv_w, k_conv_w, v_conv_w, c
             turned = [transpose_sum(h, half) for h, half in before]
             todo = jobs(pairs[k - 2]) if k >= 2 else []
             after = []
+            conv_first = k >= len(pairs) - ROPE_LAST
+            if conv_first:
+                for n, (h, half) in enumerate(current):
+                    conv_products(h, half, sums[n])
+                    conv_pairs(h, half, sums[n])
+                current = []
             for h, lo, hi in todo:
                 if h in values:
                     continue
@@ -287,10 +303,10 @@ def tile_gpt_pa_kernel(tc, x, w_words, w_scales, q_conv_w, k_conv_w, v_conv_w, c
                 counters["rope"] += 1
                 sin_product(*job)
                 r = roped.index(h)
-                if r >= len(roped) - TAIL_COS or r % COS_EVERY == COS_PHASE:
-                    cos_product(nc.vector, tables[:, 0], *job)
+                if r >= len(roped) - TAIL_COS or h % HEADS_PER_GROUP in COS_J:
+                    cos_product(True, *job)
                 else:
-                    cos_product(nc.gpsimd, cos_sb, *job)
+                    cos_product(False, *job)
                 after.append(job)
             for i, bank in late_x:
                 copy_x(i, bank, on_scalar=False)

@@ -5,7 +5,11 @@ from concourse.masks import make_identity
 
 T, C = 1024, 1024
 GROUPS, HEADS_PER_GROUP, HS = 4, 6, 128
+QUERIES_PER_GROUP = 4
+KEY, VALUE = 4, 5
 HEADS = GROUPS * HEADS_PER_GROUP
+GROUP_COLS = HEADS_PER_GROUP * HS
+TAPS = 4
 FLOPS = 2 * T * C * HEADS * HS
 
 F32 = mybir.dt.float32
@@ -22,26 +26,19 @@ P = 128
 PASSES = C // 512
 HALF = 512
 TILES = T // P
-TILES_PER_HALF = HALF // P
+HALF_TILES = HALF // P
 ROT = HS // 2
 
 EARLY_HEADS = 4
-CONV_BUFS = 4
+LAST_VALUES = 2
+COS_ON_VECTOR = (1, 3)
+THREE_TERMS = (3, 1)
+
+CONV_BUFS = EARLY_HEADS
 Y_BUFS = 6
 ROPE_BUFS = 4
 MX_BANKS = 4
 TR_BANKS = 3
-COS_EVERY = 5
-COS_PHASE = 3
-TAIL_COS = 0
-TAIL_ADD = 0
-THIRD_J = 3
-COS_J = (1, 3)
-HEAD_COS = 0
-ROPE_LAST = 0
-SPLIT_LAST = 0
-LAST_VALUES = 3
-LATE_ON_SCALAR = 2
 
 
 def tile_gpt_pa_kernel(tc, x, w_words, w_scales, q_conv_w, k_conv_w, v_conv_w, cos, sin, out_q, out_k, out_v):
@@ -51,87 +48,86 @@ def tile_gpt_pa_kernel(tc, x, w_words, w_scales, q_conv_w, k_conv_w, v_conv_w, c
         ps = ctx.enter_context(tc.psum_pool(name="ps", bufs=1))
         ctx.enter_context(tc.manual_schedule())
 
-        def tiles(pool, name, count, shape, dtype):
-            return [pool.tile(shape, dtype, name="%s%d" % (name, i), align_bytes=64) for i in range(count)]
+        def tiles(name, count, shape, dtype):
+            return [sb.tile(shape, dtype, name="%s%d" % (name, i), align_bytes=64) for i in range(count)]
 
-        x_rows = tiles(sb, "x_rows", TILES, [P, C], BF16)
-        x_t = tiles(sb, "x_t", 2, [P, PASSES, 4 * HALF], BF16)
-        x_codes = tiles(sb, "x_codes", 2, [P, PASSES, HALF], U32)
-        x_scales = tiles(sb, "x_scales", 2, [P, PASSES, HALF], U8)
-        group_cols = HEADS_PER_GROUP * HS
-        w_codes = tiles(sb, "w_codes", GROUPS, [P, PASSES, 2 * group_cols], U8)
-        plane_first = sb.tile([P, PASSES, group_cols], U8, align_bytes=64)
-        plane_rest = sb.tile([P, PASSES, (GROUPS - 1) * group_cols], U8, align_bytes=64)
-        tap_rows = sb.tile([P, 4 * HS], BF16, align_bytes=64)
-        taps = sb.tile([P, 4, HEADS], F32, align_bytes=64)
+        x_rows = tiles("x_rows", TILES, [P, C], BF16)
+        x_t = tiles("x_t", 2, [P, PASSES, 4 * HALF], BF16)
+        x_codes = tiles("x_codes", 2, [P, PASSES, HALF], U32)
+        x_scales = tiles("x_scales", 2, [P, PASSES, HALF], U8)
+        w_codes = tiles("w_codes", GROUPS, [P, PASSES, 2 * GROUP_COLS], U8)
+        scales_first = sb.tile([P, PASSES, GROUP_COLS], U8, align_bytes=64)
+        scales_rest = sb.tile([P, PASSES, (GROUPS - 1) * GROUP_COLS], U8, align_bytes=64)
+        tap_rows = sb.tile([P, TAPS * HS], BF16, align_bytes=64)
+        taps = sb.tile([P, TAPS, HEADS], F32, align_bytes=64)
         cos_sb = sb.tile([P, TILES, ROT], BF16, align_bytes=64)
         sin_sb = sb.tile([P, TILES, ROT], BF16, align_bytes=64)
         cos_wide = sb.tile([P, TILES, HS], F32, align_bytes=64)
         ident_f32 = sb.tile([P, P], F32, align_bytes=64)
         ident_bf = sb.tile([P, P], BF16, align_bytes=64)
-        prod0 = tiles(sb, "prod0", CONV_BUFS, [P, T], F32)
-        prod2 = tiles(sb, "prod2", CONV_BUFS, [P, T], F32)
-        pair01 = tiles(sb, "pair01", CONV_BUFS, [P, T], F32)
-        pair23 = tiles(sb, "pair23", CONV_BUFS, [P, T], F32)
-        y_bufs = tiles(sb, "y", Y_BUFS, [P, TILES, HS], F32)
-        y_cos = tiles(sb, "y_cos", ROPE_BUFS, [P, TILES, HS], F32)
-        y_sin = tiles(sb, "y_sin", ROPE_BUFS, [P, TILES, HS], F32)
-        rotated = tiles(sb, "rotated", ROPE_BUFS, [P, TILES, HS], F32)
+        prod0 = tiles("prod0", CONV_BUFS, [P, T], F32)
+        prod2 = tiles("prod2", CONV_BUFS, [P, T], F32)
+        pair01 = tiles("pair01", CONV_BUFS, [P, T], F32)
+        pair23 = tiles("pair23", CONV_BUFS, [P, T], F32)
+        y_bufs = tiles("y", Y_BUFS, [P, TILES, HS], F32)
+        y_cos = tiles("y_cos", ROPE_BUFS, [P, TILES, HS], F32)
+        y_sin = tiles("y_sin", ROPE_BUFS, [P, TILES, HS], F32)
+        rotated = tiles("rotated", ROPE_BUFS, [P, TILES, HS], F32)
 
         mx_banks = [ps.tile([P, HALF], F32, name="mx%d" % i) for i in range(MX_BANKS)]
         tr_banks = [ps.tile([P, HALF], F32, name="tr%d" % i) for i in range(TR_BANKS)]
         tables = ps.tile([P, 2, TILES, ROT], BF16)
 
-        nc.vector.memset(plane_first[:].bitcast(I32), 0)
+        nc.vector.memset(scales_first[:].bitcast(I32), 0)
         nc.vector.memset(tap_rows[:].bitcast(I32), 0)
         make_identity(nc, ident_f32[:])
-        nc.vector.memset(plane_rest[:].bitcast(I32), 0)
-        for i in range(CONV_BUFS):
-            nc.vector.memset(prod0[i][:, 0:1], 0.0)
-            nc.vector.memset(prod2[i][:, 0:1], 0.0)
-            nc.vector.memset(pair01[i][:, 0:2], 0.0)
+        nc.vector.memset(scales_rest[:].bitcast(I32), 0)
+        for b in range(CONV_BUFS):
+            nc.vector.memset(prod0[b][:, 0:1], 0.0)
+            nc.vector.memset(prod2[b][:, 0:1], 0.0)
+            nc.vector.memset(pair01[b][:, 0:2], 0.0)
 
         def load_x(i):
             nc.sync.dma_start(out=x_rows[i][:], in_=x[0, P * i : P * (i + 1), :])
 
-        def load_w(g):
-            src = w_words.rearrange("g p n -> p g n")[:, :, 2 * group_cols * g : 2 * group_cols * (g + 1)]
-            nc.sync.dma_start(out=w_codes[g][:].bitcast(I32), in_=src.bitcast(I32))
+        def load_codes(group):
+            src = w_words.rearrange("g p n -> p g n")[:, :, 2 * GROUP_COLS * group : 2 * GROUP_COLS * (group + 1)]
+            nc.sync.dma_start(out=w_codes[group][:].bitcast(I32), in_=src.bitcast(I32))
 
-        def load_plane(queue, plane, lo, hi):
-            for q in range(4):
-                queue.dma_start(
-                    out=plane[32 * q : 32 * q + 4, :, :].bitcast(I32),
-                    in_=w_scales[:, 4 * q : 4 * q + 4, lo:hi].rearrange("g r n -> r g n").bitcast(I32),
+        def load_scales(dst, first_col, end_col):
+            for quad in range(4):
+                nc.sync.dma_start(
+                    out=dst[32 * quad : 32 * quad + 4, :, :].bitcast(I32),
+                    in_=w_scales[:, 4 * quad : 4 * quad + 4, first_col:end_col].rearrange("g r n -> r g n").bitcast(I32),
                 )
 
-        for i in range(TILES_PER_HALF):
+        for i in range(HALF_TILES):
             load_x(i)
-        load_plane(nc.sync, plane_first, 0, group_cols)
-        load_w(0)
-        first = 0
+        load_scales(scales_first, 0, GROUP_COLS)
+        load_codes(0)
+        first_row = 0
         for conv_w in (q_conv_w, k_conv_w, v_conv_w):
-            n = conv_w.shape[0] // HS
-            nc.gpsimd.dma_start(out=tap_rows[first : first + n, :], in_=conv_w.rearrange("(h c) j -> h (c j)", c=HS))
-            first += n
+            rows = conv_w.shape[0] // HS
+            nc.gpsimd.dma_start(out=tap_rows[first_row : first_row + rows, :], in_=conv_w.rearrange("(h c) j -> h (c j)", c=HS))
+            first_row += rows
         nc.scalar.activation(out=ident_bf[:], in_=ident_f32[:], func=ACT.Copy)
-        for i in range(TILES_PER_HALF, TILES):
+        for i in range(HALF_TILES, TILES):
             load_x(i)
         nc.sync.dma_start(out=cos_sb[:], in_=cos.rearrange("(i p) d -> p i d", p=P))
         nc.sync.dma_start(out=sin_sb[:], in_=sin.rearrange("(i p) d -> p i d", p=P))
-        load_plane(nc.sync, plane_rest, group_cols, GROUPS * group_cols)
-        for g in range(1, GROUPS):
-            load_w(g)
+        load_scales(scales_rest, GROUP_COLS, GROUPS * GROUP_COLS)
+        for group in range(1, GROUPS):
+            load_codes(group)
 
-        counters = {"mx": 0, "tr": 0, "rope": 0}
+        used = {"mx": 0, "tr": 0, "rope": 0}
 
-        def take(kind, bufs):
-            buf = bufs[counters[kind] % len(bufs)]
-            counters[kind] += 1
-            return buf
+        def next_index(kind, count):
+            index = used[kind] % count
+            used[kind] += 1
+            return index
 
         def transpose_x(i):
-            bank = take("tr", tr_banks)
+            bank = tr_banks[next_index("tr", TR_BANKS)]
             words = x_rows[i][:].bitcast(F32)
             for g in range(PASSES):
                 for u in range(2):
@@ -140,7 +136,7 @@ def tile_gpt_pa_kernel(tc, x, w_words, w_scales, q_conv_w, k_conv_w, v_conv_w, c
             return bank
 
         def copy_x(i, bank, on_scalar):
-            half, j = divmod(i, TILES_PER_HALF)
+            half, j = divmod(i, HALF_TILES)
             dst = x_t[half][:].bitcast(F32).rearrange("p g (t u) -> p g t u", u=2)[:, :, P * j : P * (j + 1), :]
             src = bank[:].rearrange("p (g u t) -> p g t u", g=PASSES, u=2)
             if on_scalar:
@@ -148,50 +144,60 @@ def tile_gpt_pa_kernel(tc, x, w_words, w_scales, q_conv_w, k_conv_w, v_conv_w, c
             else:
                 nc.vector.tensor_copy(out=dst, in_=src)
 
-        def quantize_x(half, g):
-            nc.vector.quantize_mx(out=x_codes[half][:, g, :].bitcast(E5M2X4), scales=x_scales[half][:, g, :], in_=x_t[half][:, g, :])
+        def quantize_x(half):
+            for g in range(PASSES):
+                nc.vector.quantize_mx(out=x_codes[half][:, g, :].bitcast(E5M2X4), scales=x_scales[half][:, g, :], in_=x_t[half][:, g, :])
 
-        def kind_of(h):
-            g, j = divmod(h, HEADS_PER_GROUP)
-            if j < 4:
-                return out_q, 4 * g + j, 4 * g + j
-            if j == 4:
-                return out_k, g, 16 + g
-            return out_v, g, 20 + g
+        values = [h for h in range(HEADS) if h % HEADS_PER_GROUP == VALUE]
+        closing = values[GROUPS - LAST_VALUES :]
+        order = [h for h in range(HEADS) if h not in closing] + closing
+        slot = {h: i for i, h in enumerate(order)}
+        last_rotated = order[HEADS - LAST_VALUES - 1]
+        units = [(h, half) for half in range(2) for h in order[:EARLY_HEADS]]
+        units += [(h, half) for h in order[EARLY_HEADS:] for half in range(2)]
+        steps = [units[i : i + 2] for i in range(0, len(units), 2)]
 
-        def project(h, half):
-            g, j = divmod(h, HEADS_PER_GROUP)
-            bank = take("mx", mx_banks)
-            for c in range(PASSES):
-                nc.tensor.matmul_mx(
-                    out=bank[:],
-                    lhsT=w_codes[g][:, c, 2 * HS * j : 2 * HS * (j + 1)].bitcast(E2M1X4),
-                    lhsT_scale=plane_first[:, c, HS * h : HS * (h + 1)] if g == 0 else plane_rest[:, c, HS * h - group_cols : HS * (h + 1) - group_cols],
-                    rhs=x_codes[half][:, c, :].bitcast(E5M2X4),
-                    rhs_scale=x_scales[half][:, c, :],
-                    start=(c == 0),
-                    stop=(c == PASSES - 1),
-                )
-            return bank
+        def destination(h):
+            group, place = divmod(h, HEADS_PER_GROUP)
+            if place < QUERIES_PER_GROUP:
+                head = QUERIES_PER_GROUP * group + place
+                return out_q, head, head
+            first = GROUPS * QUERIES_PER_GROUP
+            if place == KEY:
+                return out_k, group, first + group
+            return out_v, group, first + GROUPS + group
 
         def tap(h, j):
-            row = kind_of(h)[2]
+            row = destination(h)[2]
             return taps[:, j, row : row + 1]
 
         def three_terms(h, half):
-            return (h % HEADS_PER_GROUP, half) == (THIRD_J, 1)
+            return (h % HEADS_PER_GROUP, half) == THREE_TERMS
 
-        def conv_products(h, half, u):
-            t0 = HALF * half
-            n = min(HALF, T - t0 - 1)
-            for buf, j in ((prod0, 0), (prod2, 2)):
-                nc.scalar.activation(out=buf[slot[h] % CONV_BUFS][:, t0 + 1 : t0 + 1 + n], in_=u[:, 0:n], func=ACT.Copy, scale=tap(h, j))
-            if three_terms(h, half):
-                nc.scalar.activation(out=pair23[slot[h] % CONV_BUFS][:, t0 : t0 + HALF], in_=u[:], func=ACT.Copy, scale=tap(h, 3))
+        def project(h, half):
+            group, place = divmod(h, HEADS_PER_GROUP)
+            bank = mx_banks[next_index("mx", MX_BANKS)]
+            scales, col = (scales_first, HS * h) if group == 0 else (scales_rest, HS * h - GROUP_COLS)
+            for g in range(PASSES):
+                nc.tensor.matmul_mx(
+                    out=bank[:],
+                    lhsT=w_codes[group][:, g, 2 * HS * place : 2 * HS * (place + 1)].bitcast(E2M1X4),
+                    lhsT_scale=scales[:, g, col : col + HS],
+                    rhs=x_codes[half][:, g, :].bitcast(E5M2X4),
+                    rhs_scale=x_scales[half][:, g, :],
+                    start=(g == 0),
+                    stop=(g == PASSES - 1),
+                )
+            return bank
 
-        def conv_pairs(h, half, u):
+        def convolve(h, half, u):
             t0 = HALF * half
             b = slot[h] % CONV_BUFS
+            n = min(HALF, T - t0 - 1)
+            for buf, j in ((prod0, 0), (prod2, 2)):
+                nc.scalar.activation(out=buf[b][:, t0 + 1 : t0 + 1 + n], in_=u[:, 0:n], func=ACT.Copy, scale=tap(h, j))
+            if three_terms(h, half):
+                nc.scalar.activation(out=pair23[b][:, t0 : t0 + HALF], in_=u[:], func=ACT.Copy, scale=tap(h, 3))
             n = min(HALF, T - t0 - 2)
             nc.vector.scalar_tensor_tensor(
                 out=pair01[b][:, t0 + 2 : t0 + 2 + n], in0=u[:, 0:n], scalar=tap(h, 1), in1=prod0[b][:, t0 : t0 + n], op0=ALU.mult, op1=ALU.add
@@ -202,34 +208,43 @@ def tile_gpt_pa_kernel(tc, x, w_words, w_scales, q_conv_w, k_conv_w, v_conv_w, c
                 )
 
         def transpose_sum(h, half):
-            bank = take("tr", tr_banks)
+            bank = tr_banks[next_index("tr", TR_BANKS)]
             b = slot[h] % CONV_BUFS
             terms = [pair01, pair23] + ([prod2] if three_terms(h, half) else [])
-            for j in range(TILES_PER_HALF):
+            for j in range(HALF_TILES):
                 t0 = HALF * half + P * j
                 for n, term in enumerate(terms):
                     nc.tensor.matmul(
-                        bank[:, P * j : P * (j + 1)], lhsT=term[b][:, t0 : t0 + P], rhs=ident_f32[:], start=(n == 0), stop=(n == len(terms) - 1), is_transpose=True
+                        bank[:, P * j : P * (j + 1)],
+                        lhsT=term[b][:, t0 : t0 + P],
+                        rhs=ident_f32[:],
+                        start=(n == 0),
+                        stop=(n == len(terms) - 1),
+                        is_transpose=True,
                     )
             return bank
 
-        def silu(h, half, bank):
-            lo = TILES_PER_HALF * half
-            nc.scalar.activation(
-                out=y_bufs[slot[h] % Y_BUFS][:, lo : lo + TILES_PER_HALF, :], in_=bank[:].rearrange("p (i d) -> p i d", d=HS), func=ACT.Silu
-            )
-
         def store(h, lo, hi, src):
-            out, head, unused = kind_of(h)
-            queue = nc.scalar if slot[h] >= HEADS - LAST_VALUES else nc.sync
+            out, head = destination(h)[:2]
+            queue = nc.scalar if h in closing else nc.sync
             queue.dma_start(out=out[0].rearrange("(i p) h d -> p i h d", p=P)[:, lo:hi, head, :], in_=src[:, lo:hi, :])
+
+        def silu(h, half, bank):
+            lo, hi = HALF_TILES * half, HALF_TILES * (half + 1)
+            y = y_bufs[slot[h] % Y_BUFS]
+            nc.scalar.activation(out=y[:, lo:hi, :], in_=bank[:].rearrange("p (i d) -> p i d", d=HS), func=ACT.Silu)
+            if h in values:
+                store(h, lo, hi, y)
 
         def both_halves(table):
             return table.rearrange("p i (o d) -> p i o d", o=1).to_broadcast([P, table.shape[1], 2, ROT])
 
-        def cos_product(on_vector, h, lo, hi, b):
+        def rope_products(h, lo, hi, b):
             y = y_bufs[slot[h] % Y_BUFS][:, lo:hi, :]
-            if on_vector:
+            s = tables[:, 1, lo:hi, :]
+            nc.vector.scalar_tensor_tensor(out=y_sin[b][:, lo:hi, 0:ROT], in0=y[:, :, ROT:HS], scalar=-1.0, in1=s, op0=ALU.mult, op1=ALU.mult)
+            nc.vector.tensor_tensor(out=y_sin[b][:, lo:hi, ROT:HS], in0=y[:, :, 0:ROT], in1=s, op=ALU.mult)
+            if h % HEADS_PER_GROUP in COS_ON_VECTOR or h == last_rotated:
                 nc.vector.tensor_tensor(
                     out=y_cos[b][:, lo:hi, :].rearrange("p i (o d) -> p i o d", o=2),
                     in0=y.rearrange("p i (o d) -> p i o d", o=2),
@@ -239,86 +254,52 @@ def tile_gpt_pa_kernel(tc, x, w_words, w_scales, q_conv_w, k_conv_w, v_conv_w, c
             else:
                 nc.gpsimd.tensor_tensor(out=y_cos[b][:, lo:hi, :], in0=y, in1=cos_wide[:, lo:hi, :], op=ALU.mult)
 
-        def sin_product(h, lo, hi, b):
-            y = y_bufs[slot[h] % Y_BUFS]
-            s = tables[:, 1, lo:hi, :]
-            nc.vector.scalar_tensor_tensor(out=y_sin[b][:, lo:hi, 0:ROT], in0=y[:, lo:hi, ROT:HS], scalar=-1.0, in1=s, op0=ALU.mult, op1=ALU.mult)
-            nc.vector.tensor_tensor(out=y_sin[b][:, lo:hi, ROT:HS], in0=y[:, lo:hi, 0:ROT], in1=s, op=ALU.mult)
-
-        def rope_add(engine, h, lo, hi, b):
-            engine.tensor_tensor(out=rotated[b][:, lo:hi, :], in0=y_cos[b][:, lo:hi, :], in1=y_sin[b][:, lo:hi, :], op=ALU.add)
+        def rope_sum(h, lo, hi, b):
+            nc.gpsimd.tensor_tensor(out=rotated[b][:, lo:hi, :], in0=y_cos[b][:, lo:hi, :], in1=y_sin[b][:, lo:hi, :], op=ALU.add)
             store(h, lo, hi, rotated[b])
 
-        def jobs(pair):
-            (h0, a), (h1, b) = pair
-            if h0 == h1 and slot[h0] < HEADS - SPLIT_LAST:
-                return [(h0, 0, TILES)]
-            return [(h, TILES_PER_HALF * half, TILES_PER_HALF * (half + 1)) for h, half in pair]
+        def rotations(step):
+            if step[0][0] in values:
+                return []
+            if step[0][0] == step[1][0] and step[0][0] != last_rotated:
+                return [(step[0][0], 0, TILES)]
+            return [(h, HALF_TILES * half, HALF_TILES * (half + 1)) for h, half in step]
 
-        values = [h for h in range(HEADS) if h % HEADS_PER_GROUP == 5]
-        order = [h for h in range(HEADS) if h not in values[GROUPS - LAST_VALUES :]] + values[GROUPS - LAST_VALUES :]
-        roped = [h for h in order if h not in values]
-        slot = {h: i for i, h in enumerate(order)}
-        units = [(h, half) for half in range(2) for h in order[:EARLY_HEADS]]
-        units += [(h, half) for h in order[EARLY_HEADS:] for half in range(2)]
-        pairs = [units[i : i + 2] for i in range(0, len(units), 2)]
-
-        for i in range(TILES_PER_HALF):
+        for i in range(HALF_TILES):
             copy_x(i, transpose_x(i), on_scalar=(i % 2 == 0))
         flat_tables = tables[:].rearrange("p s i d -> p (s i d)")
-        for j in range(4):
-            nc.tensor.transpose(flat_tables[:, P * j : P * (j + 1)], tap_rows[:, j : 4 * HS : 4], ident_bf[:])
-        nc.scalar.activation(out=taps[:], in_=flat_tables[:, 0 : 4 * P].rearrange("p (j h) -> p j h", j=4)[:, :, 0:HEADS], func=ACT.Copy)
-        for g in range(PASSES):
-            quantize_x(0, g)
-        for i in range(TILES_PER_HALF, TILES_PER_HALF + LATE_ON_SCALAR):
+        for j in range(TAPS):
+            nc.tensor.transpose(flat_tables[:, P * j : P * (j + 1)], tap_rows[:, j : TAPS * HS : TAPS], ident_bf[:])
+        nc.scalar.activation(out=taps[:], in_=flat_tables[:, 0 : TAPS * P].rearrange("p (j r) -> p j r", j=TAPS)[:, :, 0:HEADS], func=ACT.Copy)
+        quantize_x(0)
+        x_before_loop = HALF_TILES + 2
+        for i in range(HALF_TILES, x_before_loop):
             copy_x(i, transpose_x(i), on_scalar=True)
-
         nc.gpsimd.tensor_scalar(
             out=cos_wide[:].rearrange("p i (o d) -> p i o d", o=2), in0=both_halves(cos_sb[:]), scalar1=1.0, scalar2=0.0, op0=ALU.mult, op1=ALU.add
         )
-        for k in range(len(pairs) + 2):
-            current = pairs[k] if k < len(pairs) else []
-            before = pairs[k - 1] if 1 <= k <= len(pairs) else []
+
+        for k in range(len(steps) + 2):
+            current = steps[k] if k < len(steps) else []
+            previous = steps[k - 1] if 1 <= k <= len(steps) else []
             sums = [project(h, half) for h, half in current]
-            late_x = [(i, transpose_x(i)) for i in range(TILES_PER_HALF + LATE_ON_SCALAR, TILES)] if k == 0 else []
+            turned = [transpose_sum(h, half) for h, half in previous]
+            late_x = [(i, transpose_x(i)) for i in range(x_before_loop, TILES)] if k == 0 else []
             if k == 1:
-                for i, table in enumerate((cos_sb, sin_sb)):
+                for s, table in enumerate((cos_sb, sin_sb)):
                     nc.tensor.matmul(
-                        tables[:, i].rearrange("p i d -> p (i d)"), lhsT=ident_bf[:], rhs=table[:].rearrange("p i d -> p (i d)"), start=True, stop=True
+                        tables[:, s].rearrange("p i d -> p (i d)"), lhsT=ident_bf[:], rhs=table[:].rearrange("p i d -> p (i d)"), start=True, stop=True
                     )
-            turned = [transpose_sum(h, half) for h, half in before]
-            todo = jobs(pairs[k - 2]) if k >= 2 else []
-            after = []
-            conv_first = k >= len(pairs) - ROPE_LAST
-            if conv_first:
-                for n, (h, half) in enumerate(current):
-                    conv_products(h, half, sums[n])
-                    conv_pairs(h, half, sums[n])
-                current = []
-            for h, lo, hi in todo:
-                if h in values:
-                    continue
-                job = (h, lo, hi, counters["rope"] % ROPE_BUFS)
-                counters["rope"] += 1
-                sin_product(*job)
-                r = roped.index(h)
-                if r >= len(roped) - TAIL_COS or h % HEADS_PER_GROUP in COS_J:
-                    cos_product(True, *job)
-                else:
-                    cos_product(False, *job)
-                after.append(job)
-            for i, bank in late_x:
-                copy_x(i, bank, on_scalar=False)
+            jobs = [job + (next_index("rope", ROPE_BUFS),) for job in (rotations(steps[k - 2]) if k >= 2 else [])]
+            for job in jobs:
+                rope_products(*job)
             for n, (h, half) in enumerate(current):
-                conv_products(h, half, sums[n])
-                conv_pairs(h, half, sums[n])
-                if k == 0 and n == 0:
-                    for g in range(PASSES):
-                        quantize_x(1, g)
-            for job in after:
-                rope_add(nc.vector if roped.index(job[0]) >= len(roped) - TAIL_ADD else nc.gpsimd, *job)
-            for (h, half), bank in zip(before, turned):
+                convolve(h, half, sums[n])
+                if late_x and n == 0:
+                    for i, bank in late_x:
+                        copy_x(i, bank, on_scalar=True)
+                    quantize_x(1)
+            for job in jobs:
+                rope_sum(*job)
+            for (h, half), bank in zip(previous, turned):
                 silu(h, half, bank)
-                if h % HEADS_PER_GROUP == 5:
-                    store(h, TILES_PER_HALF * half, TILES_PER_HALF * (half + 1), y_bufs[slot[h] % Y_BUFS])

from contextlib import ExitStack

import concourse.mybir as mybir
from concourse.masks import make_identity

T, C = 1024, 1024
GROUPS, HEADS_PER_GROUP, HS = 4, 6, 128
QUERIES_PER_GROUP = 4
KEY, VALUE = 4, 5
HEADS = GROUPS * HEADS_PER_GROUP
GROUP_COLS = HEADS_PER_GROUP * HS
TAPS = 4
FLOPS = 2 * T * C * HEADS * HS

F32 = mybir.dt.float32
BF16 = mybir.dt.bfloat16
I32 = mybir.dt.int32
U32 = mybir.dt.uint32
U8 = mybir.dt.uint8
E5M2X4 = mybir.dt.float8_e5m2_x4
E2M1X4 = mybir.dt.float4_e2m1fn_x4
ALU = mybir.AluOpType
ACT = mybir.ActivationFunctionType

P = 128
PASSES = C // 512
HALF = 512
TILES = T // P
HALF_TILES = HALF // P
ROT = HS // 2

EARLY_HEADS = 4
LAST_VALUES = 2
COS_ON_VECTOR = (1, 3)
THREE_TERMS = (3, 1)

CONV_BUFS = EARLY_HEADS
Y_BUFS = 6
ROPE_BUFS = 4
MX_BANKS = 4
TR_BANKS = 3


def tile_gpt_pa_kernel(tc, x, w_words, w_scales, q_conv_w, k_conv_w, v_conv_w, cos, sin, out_q, out_k, out_v):
    nc = tc.nc
    with ExitStack() as ctx:
        sb = ctx.enter_context(tc.tile_pool(name="sb", bufs=1))
        ps = ctx.enter_context(tc.psum_pool(name="ps", bufs=1))
        ctx.enter_context(tc.manual_schedule())

        def tiles(name, count, shape, dtype):
            return [sb.tile(shape, dtype, name="%s%d" % (name, i), align_bytes=64) for i in range(count)]

        x_rows = tiles("x_rows", TILES, [P, C], BF16)
        x_t = tiles("x_t", 2, [P, PASSES, 4 * HALF], BF16)
        x_codes = tiles("x_codes", 2, [P, PASSES, HALF], U32)
        x_scales = tiles("x_scales", 2, [P, PASSES, HALF], U8)
        w_codes = tiles("w_codes", GROUPS, [P, PASSES, 2 * GROUP_COLS], U8)
        scales_first = sb.tile([P, PASSES, GROUP_COLS], U8, align_bytes=64)
        scales_rest = sb.tile([P, PASSES, (GROUPS - 1) * GROUP_COLS], U8, align_bytes=64)
        tap_rows = sb.tile([P, TAPS * HS], BF16, align_bytes=64)
        taps = sb.tile([P, TAPS, HEADS], F32, align_bytes=64)
        cos_sb = sb.tile([P, TILES, ROT], BF16, align_bytes=64)
        sin_sb = sb.tile([P, TILES, ROT], BF16, align_bytes=64)
        cos_wide = sb.tile([P, TILES, HS], F32, align_bytes=64)
        ident_f32 = sb.tile([P, P], F32, align_bytes=64)
        ident_bf = sb.tile([P, P], BF16, align_bytes=64)
        prod0 = tiles("prod0", CONV_BUFS, [P, T], F32)
        prod2 = tiles("prod2", CONV_BUFS, [P, T], F32)
        pair01 = tiles("pair01", CONV_BUFS, [P, T], F32)
        pair23 = tiles("pair23", CONV_BUFS, [P, T], F32)
        y_bufs = tiles("y", Y_BUFS, [P, TILES, HS], F32)
        y_cos = tiles("y_cos", ROPE_BUFS, [P, TILES, HS], F32)
        y_sin = tiles("y_sin", ROPE_BUFS, [P, TILES, HS], F32)
        rotated = tiles("rotated", ROPE_BUFS, [P, TILES, HS], F32)

        mx_banks = [ps.tile([P, HALF], F32, name="mx%d" % i) for i in range(MX_BANKS)]
        tr_banks = [ps.tile([P, HALF], F32, name="tr%d" % i) for i in range(TR_BANKS)]
        tables = ps.tile([P, 2, TILES, ROT], BF16)

        nc.vector.memset(scales_first[:].bitcast(I32), 0)
        nc.vector.memset(tap_rows[:].bitcast(I32), 0)
        make_identity(nc, ident_f32[:])
        nc.vector.memset(scales_rest[:].bitcast(I32), 0)
        for b in range(CONV_BUFS):
            nc.vector.memset(prod0[b][:, 0:1], 0.0)
            nc.vector.memset(prod2[b][:, 0:1], 0.0)
            nc.vector.memset(pair01[b][:, 0:2], 0.0)

        def load_x(i):
            nc.sync.dma_start(out=x_rows[i][:], in_=x[0, P * i : P * (i + 1), :])

        def load_codes(group):
            src = w_words.rearrange("g p n -> p g n")[:, :, 2 * GROUP_COLS * group : 2 * GROUP_COLS * (group + 1)]
            nc.sync.dma_start(out=w_codes[group][:].bitcast(I32), in_=src.bitcast(I32))

        def load_scales(dst, first_col, end_col):
            for quad in range(4):
                nc.sync.dma_start(
                    out=dst[32 * quad : 32 * quad + 4, :, :].bitcast(I32),
                    in_=w_scales[:, 4 * quad : 4 * quad + 4, first_col:end_col].rearrange("g r n -> r g n").bitcast(I32),
                )

        for i in range(HALF_TILES):
            load_x(i)
        load_scales(scales_first, 0, GROUP_COLS)
        load_codes(0)
        first_row = 0
        for conv_w in (q_conv_w, k_conv_w, v_conv_w):
            rows = conv_w.shape[0] // HS
            nc.gpsimd.dma_start(out=tap_rows[first_row : first_row + rows, :], in_=conv_w.rearrange("(h c) j -> h (c j)", c=HS))
            first_row += rows
        nc.scalar.activation(out=ident_bf[:], in_=ident_f32[:], func=ACT.Copy)
        for i in range(HALF_TILES, TILES):
            load_x(i)
        nc.sync.dma_start(out=cos_sb[:], in_=cos.rearrange("(i p) d -> p i d", p=P))
        nc.sync.dma_start(out=sin_sb[:], in_=sin.rearrange("(i p) d -> p i d", p=P))
        load_scales(scales_rest, GROUP_COLS, GROUPS * GROUP_COLS)
        for group in range(1, GROUPS):
            load_codes(group)

        used = {"mx": 0, "tr": 0, "rope": 0}

        def next_index(kind, count):
            index = used[kind] % count
            used[kind] += 1
            return index

        def transpose_x(i):
            bank = tr_banks[next_index("tr", TR_BANKS)]
            words = x_rows[i][:].bitcast(F32)
            for g in range(PASSES):
                for u in range(2):
                    col = P * (2 * g + u)
                    nc.tensor.transpose(bank[:, col : col + P], words[:, 256 * g + u : 256 * (g + 1) : 2], ident_f32[:])
            return bank

        def copy_x(i, bank, on_scalar):
            half, j = divmod(i, HALF_TILES)
            dst = x_t[half][:].bitcast(F32).rearrange("p g (t u) -> p g t u", u=2)[:, :, P * j : P * (j + 1), :]
            src = bank[:].rearrange("p (g u t) -> p g t u", g=PASSES, u=2)
            if on_scalar:
                nc.scalar.copy(out=dst, in_=src)
            else:
                nc.vector.tensor_copy(out=dst, in_=src)

        def quantize_x(half):
            for g in range(PASSES):
                nc.vector.quantize_mx(out=x_codes[half][:, g, :].bitcast(E5M2X4), scales=x_scales[half][:, g, :], in_=x_t[half][:, g, :])

        values = [h for h in range(HEADS) if h % HEADS_PER_GROUP == VALUE]
        closing = values[GROUPS - LAST_VALUES :]
        order = [h for h in range(HEADS) if h not in closing] + closing
        slot = {h: i for i, h in enumerate(order)}
        last_rotated = order[HEADS - LAST_VALUES - 1]
        units = [(h, half) for half in range(2) for h in order[:EARLY_HEADS]]
        units += [(h, half) for h in order[EARLY_HEADS:] for half in range(2)]
        steps = [units[i : i + 2] for i in range(0, len(units), 2)]

        def destination(h):
            group, place = divmod(h, HEADS_PER_GROUP)
            if place < QUERIES_PER_GROUP:
                head = QUERIES_PER_GROUP * group + place
                return out_q, head, head
            first = GROUPS * QUERIES_PER_GROUP
            if place == KEY:
                return out_k, group, first + group
            return out_v, group, first + GROUPS + group

        def tap(h, j):
            row = destination(h)[2]
            return taps[:, j, row : row + 1]

        def three_terms(h, half):
            return (h % HEADS_PER_GROUP, half) == THREE_TERMS

        def project(h, half):
            group, place = divmod(h, HEADS_PER_GROUP)
            bank = mx_banks[next_index("mx", MX_BANKS)]
            scales, col = (scales_first, HS * h) if group == 0 else (scales_rest, HS * h - GROUP_COLS)
            for g in range(PASSES):
                nc.tensor.matmul_mx(
                    out=bank[:],
                    lhsT=w_codes[group][:, g, 2 * HS * place : 2 * HS * (place + 1)].bitcast(E2M1X4),
                    lhsT_scale=scales[:, g, col : col + HS],
                    rhs=x_codes[half][:, g, :].bitcast(E5M2X4),
                    rhs_scale=x_scales[half][:, g, :],
                    start=(g == 0),
                    stop=(g == PASSES - 1),
                )
            return bank

        def convolve(h, half, u):
            t0 = HALF * half
            b = slot[h] % CONV_BUFS
            n = min(HALF, T - t0 - 1)
            for buf, j in ((prod0, 0), (prod2, 2)):
                nc.scalar.activation(out=buf[b][:, t0 + 1 : t0 + 1 + n], in_=u[:, 0:n], func=ACT.Copy, scale=tap(h, j))
            if three_terms(h, half):
                nc.scalar.activation(out=pair23[b][:, t0 : t0 + HALF], in_=u[:], func=ACT.Copy, scale=tap(h, 3))
            n = min(HALF, T - t0 - 2)
            nc.vector.scalar_tensor_tensor(
                out=pair01[b][:, t0 + 2 : t0 + 2 + n], in0=u[:, 0:n], scalar=tap(h, 1), in1=prod0[b][:, t0 : t0 + n], op0=ALU.mult, op1=ALU.add
            )
            if not three_terms(h, half):
                nc.vector.scalar_tensor_tensor(
                    out=pair23[b][:, t0 : t0 + HALF], in0=u[:], scalar=tap(h, 3), in1=prod2[b][:, t0 : t0 + HALF], op0=ALU.mult, op1=ALU.add
                )

        def transpose_sum(h, half):
            bank = tr_banks[next_index("tr", TR_BANKS)]
            b = slot[h] % CONV_BUFS
            terms = [pair01, pair23] + ([prod2] if three_terms(h, half) else [])
            for j in range(HALF_TILES):
                t0 = HALF * half + P * j
                for n, term in enumerate(terms):
                    nc.tensor.matmul(
                        bank[:, P * j : P * (j + 1)],
                        lhsT=term[b][:, t0 : t0 + P],
                        rhs=ident_f32[:],
                        start=(n == 0),
                        stop=(n == len(terms) - 1),
                        is_transpose=True,
                    )
            return bank

        def store(h, lo, hi, src):
            out, head = destination(h)[:2]
            queue = nc.scalar if h in closing else nc.sync
            queue.dma_start(out=out[0].rearrange("(i p) h d -> p i h d", p=P)[:, lo:hi, head, :], in_=src[:, lo:hi, :])

        def silu(h, half, bank):
            lo, hi = HALF_TILES * half, HALF_TILES * (half + 1)
            y = y_bufs[slot[h] % Y_BUFS]
            nc.scalar.activation(out=y[:, lo:hi, :], in_=bank[:].rearrange("p (i d) -> p i d", d=HS), func=ACT.Silu)
            if h in values:
                store(h, lo, hi, y)

        def both_halves(table):
            return table.rearrange("p i (o d) -> p i o d", o=1).to_broadcast([P, table.shape[1], 2, ROT])

        def rope_products(h, lo, hi, b):
            y = y_bufs[slot[h] % Y_BUFS][:, lo:hi, :]
            s = tables[:, 1, lo:hi, :]
            nc.vector.scalar_tensor_tensor(out=y_sin[b][:, lo:hi, 0:ROT], in0=y[:, :, ROT:HS], scalar=-1.0, in1=s, op0=ALU.mult, op1=ALU.mult)
            nc.vector.tensor_tensor(out=y_sin[b][:, lo:hi, ROT:HS], in0=y[:, :, 0:ROT], in1=s, op=ALU.mult)
            if h % HEADS_PER_GROUP in COS_ON_VECTOR or h == last_rotated:
                nc.vector.tensor_tensor(
                    out=y_cos[b][:, lo:hi, :].rearrange("p i (o d) -> p i o d", o=2),
                    in0=y.rearrange("p i (o d) -> p i o d", o=2),
                    in1=both_halves(tables[:, 0, lo:hi, :]),
                    op=ALU.mult,
                )
            else:
                nc.gpsimd.tensor_tensor(out=y_cos[b][:, lo:hi, :], in0=y, in1=cos_wide[:, lo:hi, :], op=ALU.mult)

        def rope_sum(h, lo, hi, b):
            nc.gpsimd.tensor_tensor(out=rotated[b][:, lo:hi, :], in0=y_cos[b][:, lo:hi, :], in1=y_sin[b][:, lo:hi, :], op=ALU.add)
            store(h, lo, hi, rotated[b])

        def rotations(step):
            if step[0][0] in values:
                return []
            if step[0][0] == step[1][0] and step[0][0] != last_rotated:
                return [(step[0][0], 0, TILES)]
            return [(h, HALF_TILES * half, HALF_TILES * (half + 1)) for h, half in step]

        for i in range(HALF_TILES):
            copy_x(i, transpose_x(i), on_scalar=(i % 2 == 0))
        flat_tables = tables[:].rearrange("p s i d -> p (s i d)")
        for j in range(TAPS):
            nc.tensor.transpose(flat_tables[:, P * j : P * (j + 1)], tap_rows[:, j : TAPS * HS : TAPS], ident_bf[:])
        nc.scalar.activation(out=taps[:], in_=flat_tables[:, 0 : TAPS * P].rearrange("p (j r) -> p j r", j=TAPS)[:, :, 0:HEADS], func=ACT.Copy)
        quantize_x(0)
        x_before_loop = HALF_TILES + 2
        for i in range(HALF_TILES, x_before_loop):
            copy_x(i, transpose_x(i), on_scalar=True)
        nc.gpsimd.tensor_scalar(
            out=cos_wide[:].rearrange("p i (o d) -> p i o d", o=2), in0=both_halves(cos_sb[:]), scalar1=1.0, scalar2=0.0, op0=ALU.mult, op1=ALU.add
        )

        for k in range(len(steps) + 2):
            current = steps[k] if k < len(steps) else []
            previous = steps[k - 1] if 1 <= k <= len(steps) else []
            sums = [project(h, half) for h, half in current]
            turned = [transpose_sum(h, half) for h, half in previous]
            late_x = [(i, transpose_x(i)) for i in range(x_before_loop, TILES)] if k == 0 else []
            if k == 1:
                for s, table in enumerate((cos_sb, sin_sb)):
                    nc.tensor.matmul(
                        tables[:, s].rearrange("p i d -> p (i d)"), lhsT=ident_bf[:], rhs=table[:].rearrange("p i d -> p (i d)"), start=True, stop=True
                    )
            jobs = [job + (next_index("rope", ROPE_BUFS),) for job in (rotations(steps[k - 2]) if k >= 2 else [])]
            for job in jobs:
                rope_products(*job)
            for n, (h, half) in enumerate(current):
                convolve(h, half, sums[n])
                if late_x and n == 0:
                    for i, bank in late_x:
                        copy_x(i, bank, on_scalar=True)
                    quantize_x(1)
            for job in jobs:
                rope_sum(*job)
            for (h, half), bank in zip(previous, turned):
                silu(h, half, bank)
